import numpy as np
import ml_dtypes


def mxq(x, axis, fmt="e4m3"):
    dtype, down = {"e4m3": (ml_dtypes.float8_e4m3fn, 7), "e5m2": (ml_dtypes.float8_e5m2, 14)}[fmt]
    v = np.moveaxis(np.asarray(x, np.float32).astype(ml_dtypes.bfloat16).astype(np.float64), axis, -1)
    blocks = v.reshape(v.shape[:-1] + (-1, 32))
    amax = np.abs(blocks).max(-1, keepdims=True)
    byte = np.maximum(np.where(amax > 0, np.frexp(amax)[1] - 1 + 127, 0) - down, 1)
    scale = np.exp2(byte - 127.0)
    codes = (blocks / scale).astype(np.float32).astype(dtype).astype(np.float64)
    return np.moveaxis((codes * scale).reshape(v.shape), -1, axis)


WIDE = False


def mx_kscale(k):
    if not WIDE:
        return np.ones(k)
    levels = np.array([18, -18])
    if k % 512:
        return np.exp2(np.random.permutation(np.resize(levels, k // 32))).repeat(32)
    a = np.empty((k // 512, 16))
    for p in range(k // 512):
        a[p, :8] = np.random.permutation(np.resize(levels, 8))
        for g in range(8):
            far = levels[np.abs(levels - a[p, g]) >= 10]
            a[p, g + 8] = far[np.random.randint(len(far))]
    return np.exp2(a.ravel()).repeat(32)


BF16 = ml_dtypes.bfloat16


def bf(x):
    return np.asarray(x, np.float32).astype(BF16)


def f64(x):
    return np.asarray(x).astype(np.float64)


N, E, H = 2048, 512, 512


def draw_adj():
    p = np.random.standard_normal(N)
    return np.exp(1.5 * np.random.standard_normal((N, N)) + 0.5 * p[:, None] + 0.5 * p[None, :]) * 0.3 / N


def setup_inputs():
    u = mx_kscale(N)
    v = mx_kscale(H)
    s = mx_kscale(N)
    h0 = bf(np.maximum(np.random.standard_normal((N, E)), 0.0))
    a0 = bf(draw_adj())
    w = np.random.standard_normal((E, H)) * 1.5 / np.sqrt(E)
    w0 = bf(w - w.mean(axis=0))
    b = bf(np.random.standard_normal(H) * 0.1)
    dis = f64(a0).sum(axis=1) ** -0.5
    z2 = dis[:, None] * (f64(a0) @ (dis[:, None] * (f64(h0) @ f64(w0)))) + f64(b)
    g = bf(np.random.standard_normal((N, H)) * np.exp2(np.random.randint(-6, 1, (N, 1))) * 16.0 * u[:, None] * v)
    return {"h_enc": bf(f64(h0) * s[:, None]),
            "adj": bf(f64(a0) / u[:, None] / s),
            "gcn1_w": bf(f64(w0) / v),
            "gcn1_b": b,
            "dis": np.asarray(dis, np.float32),
            "z2": np.asarray(z2, np.float32),
            "grad_out": g}


def reference(h_enc, adj, gcn1_w, gcn1_b, dis, z2, grad_out):
    d = f64(dis)[:, None]
    dz2 = d * f64(grad_out) * (f64(z2) > 0.0)
    dy = mxq(f64(adj), 0, "e4m3").T @ mxq(dz2, 0, "e5m2")
    dz1 = d * dy
    dh_enc = mxq(dz1, 1, "e5m2") @ mxq(f64(gcn1_w), 1, "e4m3").T
    dw = mxq(f64(h_enc), 0, "e4m3").T @ mxq(dz1, 0, "e5m2")
    return dh_enc, dw

@@ -1,0 +1,408 @@
+from contextlib import ExitStack
+
+import concourse.mybir as mybir
+from concourse.masks import make_identity
+
+N, E, H = 2048, 512, 512
+
+FLOPS = 2 * N * N * H + 2 * N * H * E + 2 * N * E * H
+BYTES = 2 * (N * E + N * N + E * H + N * H) + 4 * (N + N * H) + 4 * (N * E + E * H)
+
+F32 = mybir.dt.float32
+BF16 = mybir.dt.bfloat16
+U32 = mybir.dt.uint32
+U8 = mybir.dt.uint8
+E4M3 = mybir.dt.float8_e4m3fn_x4
+E5M2 = mybir.dt.float8_e5m2_x4
+ALU = mybir.AluOpType
+COPY = mybir.ActivationFunctionType.Copy
+
+P = 128
+K4 = 4
+G = 512
+RG = N // G
+
+
+def tile_gcnclassifer_pa_v_kernel(tc, h_enc, adj, gcn1_w, gcn1_b, dis, z2, grad_out, out_0, out_1):
+    nc = tc.nc
+    with ExitStack() as ctx:
+        const = ctx.enter_context(tc.tile_pool(name="const", bufs=1))
+        rawp = ctx.enter_context(tc.tile_pool(name="rawp", bufs=4))
+        work = ctx.enter_context(tc.tile_pool(name="work", bufs=2))
+        code = ctx.enter_context(tc.tile_pool(name="code", bufs=4))
+        psum = ctx.enter_context(tc.psum_pool(name="psum", bufs=1))
+
+        ident = const.tile([P, P], F32, name="ident")
+        make_identity(nc, ident[:])
+        dummy = const.tile([P, 8], F32, name="dummy")
+        nc.vector.memset(dummy[:], 0.0)
+        nc.scalar.activation(out=dummy[:, 0:1], in_=dummy[:, 1:2], func=COPY)
+
+        def bank(b, name):
+            return psum.tile([P, G], F32, name=name, tag="b%d" % b)
+
+        dis_i = const.tile([P, RG, K4], F32, name="dis_i")
+        dis_j = const.tile([P, RG, 4], F32, name="dis_j")
+        dis_x = const.tile([P, RG, 16], F32, name="dis_x")
+        dis_p = const.tile([P, RG, 4, 4], F32, name="dis_p")
+        pick = const.tile([P, 4], F32, name="pick")
+        z2_raw, g_raw, adj_raw, h_raw = {}, {}, {}, {}
+
+        def load_g(r):
+            t = rawp.tile([P, K4, G], BF16, name="g_raw", tag="gh", bufs=4)
+            nc.sync.dma_start(out=t[:], in_=grad_out[r * G : (r + 1) * G, :].rearrange("(p i) c -> p i c", i=K4))
+            g_raw[r] = t
+
+        def load_z2(r):
+            t = rawp.tile([P, K4, G], F32, name="z2_raw", tag="z2", bufs=4)
+            nc.sync.dma_start(out=t[:], in_=z2[r * G : (r + 1) * G, :].rearrange("(p i) c -> p i c", i=K4))
+            z2_raw[r] = t
+
+        def adj_tile(half, r):
+            t = rawp.tile([P, K4, 2 * G], BF16, name="adj_raw", tag="adj", bufs=6)
+            adj_raw[half, r] = t
+            return t
+
+        def load_adj(half, r, lo=0, hi=2 * G):
+            rows = adj[r * G : (r + 1) * G, half * 2 * G + lo : half * 2 * G + hi]
+            nc.sync.dma_start(out=adj_raw[half, r][:, :, lo:hi], in_=rows.rearrange("(p i) c -> p i c", i=K4))
+
+        def load_h(g):
+            t = rawp.tile([P, K4, G], BF16, name="h_raw", tag="gh", bufs=4)
+            rows = h_enc[g * G : (g + 1) * G, :].rearrange("(a t r) c -> t a r c", t=4, r=4)
+            for s in range(4):
+                nc.sync.dma_start(out=t[:, s, :], in_=rows[s])
+            h_raw[g] = t
+
+        stage = {}
+
+        def stage_tile(key):
+            t = work.tile([P, 4 * G], BF16, name="stage", tag="stage", bufs=7, align_bytes=64)
+            stage[key] = t
+            return t
+
+        codes = {}
+
+        def quantize(key, fmt, tag, bufs, width=G, src=None):
+            cw = code.tile([P, width], U32, name="cw_" + tag, tag="c_" + tag, bufs=bufs, align_bytes=64)
+            sc = code.tile([P, width], U8, name="sc_" + tag, tag="s_" + tag, bufs=bufs, align_bytes=64)
+            nc.vector.quantize_mx(out=cw[:].bitcast(fmt), scales=sc[:], in_=(stage[key][:] if src is None else src))
+            codes[key] = (cw, sc)
+
+        def copy(eng, out, in_):
+            if eng == "v":
+                nc.vector.tensor_copy(out=out, in_=in_)
+            else:
+                nc.scalar.copy(out=out, in_=in_)
+
+        def int_adj(eng, q, r):
+            raw = adj_raw[q // 2, r][:, :, (q % 2) * G : (q % 2 + 1) * G]
+            dst = stage_tile(("adj", q, r))
+            copy(eng, dst[:].rearrange("p (t a r i) -> p t a i r", t=4, r=4, i=K4), raw.rearrange("p i (a t r) -> p t a i r", t=4, r=4))
+
+        def q_adj(q, r):
+            quantize(("adj", q, r), E4M3, "adj", 10)
+
+        def int_h(eng, g):
+            dst = stage_tile(("h", g))
+            copy(eng, dst[:].rearrange("p (c i t) -> p c t i", i=4, t=K4), h_raw[g][:].rearrange("p t (c i) -> p c t i", i=4))
+
+        def q_h(g):
+            quantize(("h", g), E4M3, "h", 4)
+
+        scaled = {}
+
+        def scale_g(r):
+            t = work.tile([P, K4, G], F32, name="scaled", tag="scaled", bufs=1)
+            for i in range(K4):
+                nc.scalar.activation(out=t[:, i, :], in_=g_raw[r][:, i, :], func=COPY, scale=dis_i[:, r, i : i + 1])
+            scaled[r] = t
+
+        def mask(r):
+            dst = stage_tile(("dz2", r))
+            nc.vector.scalar_tensor_tensor(
+                out=dst[:].rearrange("p (c i) -> p c i", i=K4),
+                in0=z2_raw[r][:].rearrange("p i c -> p c i"),
+                scalar=0.0,
+                in1=scaled[r][:].rearrange("p i c -> p c i"),
+                op0=ALU.is_gt,
+                op1=ALU.mult,
+            )
+
+        def q_dz2(r):
+            quantize(("dz2", r), E5M2, "dz2", 4)
+
+        dy = {}
+        dy_bank = {0: 0, 1: 4, 2: 4, 3: 4}
+
+        def dy_pass(q, r):
+            for t in range(4):
+                if r == 0:
+                    dy[q, t] = bank(dy_bank[q] + t, "dy")
+                a, asc = codes["adj", q, r]
+                b, bsc = codes["dz2", r]
+                m = slice(t * P, (t + 1) * P)
+                nc.tensor.matmul_mx(
+                    out=dy[q, t][:], lhsT=a[:, m].bitcast(E4M3), lhsT_scale=asc[:, m],
+                    rhs=b[:].bitcast(E5M2), rhs_scale=bsc[:], start=(r == 0), stop=(r == RG - 1))
+
+        dz1 = {}
+
+        def e1(eng, q, t):
+            if t == 0:
+                dz1[q] = work.tile([P, 4, G], BF16, name="dz1", tag="dz1", bufs=2, align_bytes=64)
+            s = dis_j[:, q, t : t + 1]
+            if eng == "v":
+                nc.vector.tensor_scalar(out=dz1[q][:, t, :], in0=dy[q, t][:], scalar1=s, scalar2=None, op0=ALU.mult)
+            else:
+                nc.scalar.activation(out=dz1[q][:, t, :], in_=dy[q, t][:], func=COPY, scale=s)
+
+        def int_dz1(eng, q):
+            dst = stage_tile(("dz1", q))
+            copy(eng, dst[:].rearrange("p (c i t) -> p c t i", i=4, t=4), dz1[q][:].rearrange("p t (c i) -> p c t i", i=4))
+
+        def q_dz1(q):
+            quantize(("dz1", q), E5M2, "dz1", 4)
+
+        xt = {}
+
+        def transpose_dz1(q, pair):
+            x = bank(pair, "xt")
+            xt[q, pair] = x
+            xv = x[:].rearrange("p (s u m) -> p s u m", s=2, u=2)
+            for s in range(2):
+                words = dz1[q][:, 2 * pair + s, :].bitcast(F32)
+                for u in range(2):
+                    nc.tensor.transpose(xv[:, s, u, :], words[:, u::2], ident[:])
+
+        def e2(eng, q, pair):
+            t = work.tile([P, 8 * P], BF16, name="dz1t", tag="dz1t", bufs=3, align_bytes=64)
+            copy(eng, t[:].bitcast(F32).rearrange("p (s m u) -> p s m u", s=2, u=2), xt[q, pair][:].rearrange("p (s u m) -> p s m u", s=2, u=2))
+            stage["dz1t", q, pair] = t
+
+        def q_dz1t(q, pair):
+            quantize(("dz1t", q, pair), E5M2, "dz1t", 4, width=2 * P)
+
+        o0 = {}
+
+        def out0_pass(q, t):
+            o0[q, t] = bank(2 + t % 2, "o0")
+            a, asc = codes["dz1t", q, t // 2]
+            b, bsc = codes["w"]
+            m = slice((t % 2) * P, (t % 2 + 1) * P)
+            nc.tensor.matmul_mx(
+                out=o0[q, t][:], lhsT=a[:, m].bitcast(E5M2), lhsT_scale=asc[:, m],
+                rhs=b[:].bitcast(E4M3), rhs_scale=bsc[:], start=True, stop=True)
+
+        def e3(eng, q, t):
+            o = work.tile([P, G], F32, name="o_sb", tag="o_sb", bufs=5)
+            copy(eng, o[:], o0[q, t][:])
+            rows = out_0[q * G : (q + 1) * G, :].rearrange("(a t r) c -> t a r c", t=4, r=4)
+            nc.sync.dma_start(out=rows[t], in_=o[:])
+
+        o1 = {}
+
+        def out1_pass(e, g):
+            if g == 0:
+                o1[e] = bank(4 + e, "o1")
+            a, asc = codes["h", g]
+            b, bsc = codes["dz1", g]
+            m = slice(e * P, (e + 1) * P)
+            nc.tensor.matmul_mx(
+                out=o1[e][:], lhsT=a[:, m].bitcast(E4M3), lhsT_scale=asc[:, m],
+                rhs=b[:].bitcast(E5M2), rhs_scale=bsc[:], start=(g == 0), stop=(g == RG - 1))
+
+        def e4(eng, e):
+            o = work.tile([P, G], F32, name="o_sb", tag="o_sb", bufs=5)
+            copy(eng, o[:], o1[e][:])
+            nc.sync.dma_start(out=out_1[e * P : (e + 1) * P, :], in_=o[:])
+
+        ctx.enter_context(tc.manual_schedule())
+        nc.scalar.dma_start(out=dis_i[:], in_=dis.rearrange("(g p i) -> p g i", g=RG, i=K4))
+        for g in range(RG):
+            src = dis[g * G : (g + 1) * G].rearrange("(a x) -> a x", x=16)
+            nc.scalar.dma_start(out=dis_x[:, g, :], in_=src.unsqueeze(1).to_broadcast([32, 4, 16]))
+        nc.vector.tensor_reduce(out=pick[:], in_=ident[:].rearrange("p (a r) -> p r a", r=4), axis=mybir.AxisListType.X, op=ALU.add)
+
+        adj_tile(0, 0)
+        load_adj(0, 0, 0, G)
+        load_g(0)
+        load_adj(0, 0, G, 2 * G)
+        load_z2(0)
+        w_raw = const.tile([P, 4, H], BF16, name="w_raw", align_bytes=64)
+        nc.sync.dma_start(out=w_raw[:], in_=gcn1_w.rearrange("(e p) c -> p e c", p=P))
+        for r in range(1, RG):
+            load_g(r)
+            adj_tile(0, r)
+            load_adj(0, r)
+            load_z2(r)
+        for r in range(2):
+            adj_tile(1, r)
+            load_adj(1, r)
+
+        w_grp = const.tile([P, 4 * E], BF16, name="w_grp", align_bytes=64)
+
+        def transpose_w(pair):
+            x = bank(6 + pair, "xw")
+            xt["w", pair] = x
+            xv = x[:].rearrange("p (s u m) -> p s u m", s=2, u=2)
+            for s in range(2):
+                words = w_raw[:, 2 * pair + s, :].bitcast(F32)
+                for u in range(2):
+                    nc.tensor.transpose(xv[:, s, u, :], words[:, u::2], ident[:])
+
+        def e_w(eng, pair):
+            dst = w_grp[:].bitcast(F32)[:, pair * 512 : (pair + 1) * 512]
+            copy(eng, dst.rearrange("p (s m u) -> p s m u", s=2, u=2), xt["w", pair][:].rearrange("p (s u m) -> p s m u", s=2, u=2))
+
+        for r in range(RG):
+            int_adj("v", 0, r)
+            scale_g(r)
+            int_adj("s", 1, r)
+            if r > 0:
+                q_dz2(r - 1)
+                q_adj(1, r - 1)
+                dy_pass(0, r - 1)
+            if r == 1:
+                nc.vector.tensor_tensor(
+                    out=dis_p[:].rearrange("p g t r -> p (g t) r"), in0=dis_x[:].rearrange("p g (t r) -> p (g t) r", r=4),
+                    in1=pick[:].unsqueeze(1).to_broadcast([P, 16, 4]), op=ALU.mult)
+                nc.vector.tensor_reduce(out=dis_j[:].rearrange("p g t -> p (g t)"), in_=dis_p[:].rearrange("p g t r -> p (g t) r"), axis=mybir.AxisListType.X, op=ALU.add)
+                transpose_w(0)
+                transpose_w(1)
+            if r == 2:
+                e_w("s", 0)
+                e_w("v", 1)
+                quantize("w", E4M3, "w", 1, src=w_grp[:])
+                dy_pass(1, 0)
+            if r > 1:
+                dy_pass(1, r - 1)
+            q_adj(0, r)
+            mask(r)
+        for r in range(2, RG):
+            adj_tile(1, r)
+            load_adj(1, r)
+        for g in range(RG):
+            load_h(g)
+
+        int_adj("v", 2, 0)
+        q_dz2(3)
+        q_adj(1, 3)
+        dy_pass(0, 3)
+        dy_pass(1, 3)
+        for t in range(4):
+            e1("s", 0, t)
+        q_adj(2, 0)
+        int_adj("v", 2, 1)
+        transpose_dz1(0, 0)
+        transpose_dz1(0, 1)
+        e2("s", 0, 0)
+        e2("s", 0, 1)
+        int_dz1("v", 0)
+        q_adj(2, 1)
+        q_dz1t(0, 0)
+        q_dz1t(0, 1)
+        for t in range(4):
+            e1("s", 1, t)
+        q_dz1(0)
+        for t in range(2):
+            out0_pass(0, t)
+        int_adj("v", 2, 2)
+        dy_pass(2, 0)
+        dy_pass(2, 1)
+        e3("s", 0, 0)
+        e3("s", 0, 1)
+        for t in range(2, 4):
+            out0_pass(0, t)
+        transpose_dz1(1, 0)
+        transpose_dz1(1, 1)
+        e3("s", 0, 2)
+        e3("s", 0, 3)
+        e2("s", 1, 0)
+        e2("s", 1, 1)
+        int_dz1("v", 1)
+        q_adj(2, 2)
+        dy_pass(2, 2)
+        q_dz1t(1, 0)
+        q_dz1t(1, 1)
+        int_adj("s", 2, 3)
+        for t in range(2):
+            out0_pass(1, t)
+        q_dz1(1)
+        int_adj("v", 3, 0)
+        e3("s", 1, 0)
+        e3("s", 1, 1)
+        for t in range(2, 4):
+            out0_pass(1, t)
+        q_adj(2, 3)
+        dy_pass(2, 3)
+        e3("s", 1, 2)
+        e3("s", 1, 3)
+        int_adj("v", 3, 1)
+        q_adj(3, 0)
+        for t in range(4):
+            e1("s", 2, t)
+        int_h("v", 0)
+        q_adj(3, 1)
+        transpose_dz1(2, 0)
+        transpose_dz1(2, 1)
+        e2("s", 2, 0)
+        e2("s", 2, 1)
+        dy_pass(3, 0)
+        dy_pass(3, 1)
+        int_dz1("v", 2)
+        q_h(0)
+        int_adj("s", 3, 3)
+        q_dz1t(2, 0)
+        q_dz1t(2, 1)
+        int_adj("v", 3, 2)
+        q_dz1(2)
+        for t in range(2):
+            out0_pass(2, t)
+        int_h("v", 1)
+        q_adj(3, 2)
+        dy_pass(3, 2)
+        e3("s", 2, 0)
+        e3("s", 2, 1)
+        for t in range(2, 4):
+            out0_pass(2, t)
+        q_adj(3, 3)
+        dy_pass(3, 3)
+        q_h(1)
+        int_h("s", 3)
+        int_h("v", 2)
+        e3("s", 2, 2)
+        e3("s", 2, 3)
+        e1("s", 3, 0)
+        e1("v", 3, 1)
+        e1("s", 3, 2)
+        e1("v", 3, 3)
+        q_h(2)
+        transpose_dz1(3, 0)
+        transpose_dz1(3, 1)
+        for g in range(2):
+            for e in range(4):
+                out1_pass(e, g)
+        for e in range(4):
+            out1_pass(e, 2)
+        e2("s", 3, 0)
+        e2("s", 3, 1)
+        int_dz1("v", 3)
+        q_h(3)
+        q_dz1t(3, 0)
+        q_dz1t(3, 1)
+        q_dz1(3)
+        for t in range(2):
+            out0_pass(3, t)
+        for e in range(4):
+            out1_pass(e, 3)
+        e3("s", 3, 0)
+        e3("v", 3, 1)
+        for t in range(2, 4):
+            out0_pass(3, t)
+        e4("s", 0)
+        e4("v", 1)
+        e4("s", 2)
+        e4("v", 3)
+        e3("s", 3, 2)
+        e3("v", 3, 3)

@@ -58,14 +58,19 @@ def tile_gcnclassifer_pa_v_kernel(tc, h_enc, adj, gcn1_w, gcn1_b, dis, z2, grad_
             nc.sync.dma_start(out=t[:], in_=z2[r * G : (r + 1) * G, :].rearrange("(p i) c -> p i c", i=K4))
             z2_raw[r] = t
 
-        def adj_tile(half, r):
-            t = rawp.tile([P, K4, 2 * G], BF16, name="adj_raw", tag="adj", bufs=6)
-            adj_raw[half, r] = t
-            return t
+        def load_adj(q, r):
+            n = 1 if q < 2 else 2
+            t = rawp.tile([P, K4, n * G], BF16, name="adj_raw", tag="adj%d" % n, bufs=(6 if n == 1 else 4))
+            rows = adj[r * G : (r + 1) * G, q * G : (q + n) * G]
+            nc.sync.dma_start(out=t[:], in_=rows.rearrange("(p i) c -> p i c", i=K4))
+            for s in range(n):
+                adj_raw[q + s, r] = t[:, :, s * G : (s + 1) * G]
 
-        def load_adj(half, r, lo=0, hi=2 * G):
-            rows = adj[r * G : (r + 1) * G, half * 2 * G + lo : half * 2 * G + hi]
-            nc.sync.dma_start(out=adj_raw[half, r][:, :, lo:hi], in_=rows.rearrange("(p i) c -> p i c", i=K4))
+        w_raw = const.tile([P, 4, H], BF16, name="w_raw", align_bytes=64)
+        w_grp = const.tile([P, 4 * E], BF16, name="w_grp", align_bytes=64)
+
+        def load_w():
+            nc.sync.dma_start(out=w_raw[:], in_=gcn1_w.rearrange("(e p) c -> p e c", p=P))
 
         def load_h(g):
             t = rawp.tile([P, K4, G], BF16, name="h_raw", tag="gh", bufs=4)
@@ -96,12 +101,12 @@ def tile_gcnclassifer_pa_v_kernel(tc, h_enc, adj, gcn1_w, gcn1_b, dis, z2, grad_
                 nc.scalar.copy(out=out, in_=in_)
 
         def int_adj(eng, q, r):
-            raw = adj_raw[q // 2, r][:, :, (q % 2) * G : (q % 2 + 1) * G]
+            raw = adj_raw[q, r]
             dst = stage_tile(("adj", q, r))
             copy(eng, dst[:].rearrange("p (t a r i) -> p t a i r", t=4, r=4, i=K4), raw.rearrange("p i (a t r) -> p t a i r", t=4, r=4))
 
         def q_adj(q, r):
-            quantize(("adj", q, r), E4M3, "adj", 10)
+            quantize(("adj", q, r), E4M3, "adj", 8)
 
         def int_h(eng, g):
             dst = stage_tile(("h", g))
@@ -110,30 +115,24 @@ def tile_gcnclassifer_pa_v_kernel(tc, h_enc, adj, gcn1_w, gcn1_b, dis, z2, grad_
         def q_h(g):
             quantize(("h", g), E4M3, "h", 4)
 
-        scaled = {}
-
-        def scale_g(r):
-            t = work.tile([P, K4, G], F32, name="scaled", tag="scaled", bufs=1)
+        def md(r):
             for i in range(K4):
-                nc.scalar.activation(out=t[:, i, :], in_=g_raw[r][:, i, :], func=COPY, scale=dis_i[:, r, i : i + 1])
-            scaled[r] = t
+                nc.vector.tensor_scalar(
+                    out=z2_raw[r][:, i, :], in0=z2_raw[r][:, i, :], scalar1=0.0, scalar2=dis_i[:, r, i : i + 1], op0=ALU.is_gt, op1=ALU.mult)
 
-        def mask(r):
+        def dz2(r):
             dst = stage_tile(("dz2", r))
-            nc.vector.scalar_tensor_tensor(
-                out=dst[:].rearrange("p (c i) -> p c i", i=K4),
-                in0=z2_raw[r][:].rearrange("p i c -> p c i"),
-                scalar=0.0,
-                in1=scaled[r][:].rearrange("p i c -> p c i"),
-                op0=ALU.is_gt,
-                op1=ALU.mult,
-            )
+            nc.vector.tensor_tensor(
+                out=dst[:].rearrange("p (c i t) -> p c t i", i=4, t=K4),
+                in0=z2_raw[r][:].rearrange("p t (c i) -> p c t i", i=4),
+                in1=g_raw[r][:].rearrange("p t (c i) -> p c t i", i=4),
+                op=ALU.mult)
 
         def q_dz2(r):
             quantize(("dz2", r), E5M2, "dz2", 4)
 
         dy = {}
-        dy_bank = {0: 0, 1: 4, 2: 4, 3: 4}
+        dy_bank = [0, 4, 0, 4]
 
         def dy_pass(q, r):
             for t in range(4):
@@ -167,7 +166,7 @@ def tile_gcnclassifer_pa_v_kernel(tc, h_enc, adj, gcn1_w, gcn1_b, dis, z2, grad_
         xt = {}
 
         def transpose_dz1(q, pair):
-            x = bank(pair, "xt")
+            x = bank(dy_bank[q] + pair, "xt")
             xt[q, pair] = x
             xv = x[:].rearrange("p (s u m) -> p s u m", s=2, u=2)
             for s in range(2):
@@ -176,7 +175,7 @@ def tile_gcnclassifer_pa_v_kernel(tc, h_enc, adj, gcn1_w, gcn1_b, dis, z2, grad_
                     nc.tensor.transpose(xv[:, s, u, :], words[:, u::2], ident[:])
 
         def e2(eng, q, pair):
-            t = work.tile([P, 8 * P], BF16, name="dz1t", tag="dz1t", bufs=3, align_bytes=64)
+            t = work.tile([P, 8 * P], BF16, name="dz1t", tag="dz1t", bufs=4, align_bytes=64)
             copy(eng, t[:].bitcast(F32).rearrange("p (s m u) -> p s m u", s=2, u=2), xt[q, pair][:].rearrange("p (s u m) -> p s m u", s=2, u=2))
             stage["dz1t", q, pair] = t
 
@@ -186,7 +185,7 @@ def tile_gcnclassifer_pa_v_kernel(tc, h_enc, adj, gcn1_w, gcn1_b, dis, z2, grad_
         o0 = {}
 
         def out0_pass(q, t):
-            o0[q, t] = bank(2 + t % 2, "o0")
+            o0[q, t] = bank(dy_bank[q] + (t + 2) % 4, "o0")
             a, asc = codes["dz1t", q, t // 2]
             b, bsc = codes["w"]
             m = slice((t % 2) * P, (t % 2 + 1) * P)
@@ -195,7 +194,7 @@ def tile_gcnclassifer_pa_v_kernel(tc, h_enc, adj, gcn1_w, gcn1_b, dis, z2, grad_
                 rhs=b[:].bitcast(E4M3), rhs_scale=bsc[:], start=True, stop=True)
 
         def e3(eng, q, t):
-            o = work.tile([P, G], F32, name="o_sb", tag="o_sb", bufs=5)
+            o = work.tile([P, G], F32, name="o_sb", tag="o_sb", bufs=8)
             copy(eng, o[:], o0[q, t][:])
             rows = out_0[q * G : (q + 1) * G, :].rearrange("(a t r) c -> t a r c", t=4, r=4)
             nc.sync.dma_start(out=rows[t], in_=o[:])
@@ -204,7 +203,7 @@ def tile_gcnclassifer_pa_v_kernel(tc, h_enc, adj, gcn1_w, gcn1_b, dis, z2, grad_
 
         def out1_pass(e, g):
             if g == 0:
-                o1[e] = bank(4 + e, "o1")
+                o1[e] = bank(e, "o1")
             a, asc = codes["h", g]
             b, bsc = codes["dz1", g]
             m = slice(e * P, (e + 1) * P)
@@ -213,34 +212,15 @@ def tile_gcnclassifer_pa_v_kernel(tc, h_enc, adj, gcn1_w, gcn1_b, dis, z2, grad_
                 rhs=b[:].bitcast(E5M2), rhs_scale=bsc[:], start=(g == 0), stop=(g == RG - 1))
 
         def e4(eng, e):
-            o = work.tile([P, G], F32, name="o_sb", tag="o_sb", bufs=5)
+            o = work.tile([P, G], F32, name="o_sb", tag="o_sb", bufs=8)
             copy(eng, o[:], o1[e][:])
             nc.sync.dma_start(out=out_1[e * P : (e + 1) * P, :], in_=o[:])
 
-        ctx.enter_context(tc.manual_schedule())
-        nc.scalar.dma_start(out=dis_i[:], in_=dis.rearrange("(g p i) -> p g i", g=RG, i=K4))
-        for g in range(RG):
-            src = dis[g * G : (g + 1) * G].rearrange("(a x) -> a x", x=16)
-            nc.scalar.dma_start(out=dis_x[:, g, :], in_=src.unsqueeze(1).to_broadcast([32, 4, 16]))
-        nc.vector.tensor_reduce(out=pick[:], in_=ident[:].rearrange("p (a r) -> p r a", r=4), axis=mybir.AxisListType.X, op=ALU.add)
-
-        adj_tile(0, 0)
-        load_adj(0, 0, 0, G)
-        load_g(0)
-        load_adj(0, 0, G, 2 * G)
-        load_z2(0)
-        w_raw = const.tile([P, 4, H], BF16, name="w_raw", align_bytes=64)
-        nc.sync.dma_start(out=w_raw[:], in_=gcn1_w.rearrange("(e p) c -> p e c", p=P))
-        for r in range(1, RG):
-            load_g(r)
-            adj_tile(0, r)
-            load_adj(0, r)
-            load_z2(r)
-        for r in range(2):
-            adj_tile(1, r)
-            load_adj(1, r)
-
-        w_grp = const.tile([P, 4 * E], BF16, name="w_grp", align_bytes=64)
+        def dis_j_pick():
+            nc.vector.tensor_tensor(
+                out=dis_p[:].rearrange("p g t r -> p (g t) r"), in0=dis_x[:].rearrange("p g (t r) -> p (g t) r", r=4),
+                in1=pick[:].unsqueeze(1).to_broadcast([P, 16, 4]), op=ALU.mult)
+            nc.vector.tensor_reduce(out=dis_j[:].rearrange("p g t -> p (g t)"), in_=dis_p[:].rearrange("p g t r -> p (g t) r"), axis=mybir.AxisListType.X, op=ALU.add)
 
         def transpose_w(pair):
             x = bank(6 + pair, "xw")
@@ -255,154 +235,94 @@ def tile_gcnclassifer_pa_v_kernel(tc, h_enc, adj, gcn1_w, gcn1_b, dis, z2, grad_
             dst = w_grp[:].bitcast(F32)[:, pair * 512 : (pair + 1) * 512]
             copy(eng, dst.rearrange("p (s m u) -> p s m u", s=2, u=2), xt["w", pair][:].rearrange("p (s u m) -> p s m u", s=2, u=2))
 
+        def q_w():
+            quantize("w", E4M3, "w", 1, src=w_grp[:])
+
+        ctx.enter_context(tc.manual_schedule())
+        nc.scalar.dma_start(out=dis_i[:], in_=dis.rearrange("(g p i) -> p g i", g=RG, i=K4))
+        for g in range(RG):
+            src = dis[g * G : (g + 1) * G].rearrange("(a x) -> a x", x=16)
+            nc.scalar.dma_start(out=dis_x[:, g, :], in_=src.unsqueeze(1).to_broadcast([32, 4, 16]))
+        nc.vector.tensor_reduce(out=pick[:], in_=ident[:].rearrange("p (a r) -> p r a", r=4), axis=mybir.AxisListType.X, op=ALU.add)
         for r in range(RG):
-            int_adj("v", 0, r)
-            scale_g(r)
-            int_adj("s", 1, r)
-            if r > 0:
-                q_dz2(r - 1)
-                q_adj(1, r - 1)
-                dy_pass(0, r - 1)
-            if r == 1:
-                nc.vector.tensor_tensor(
-                    out=dis_p[:].rearrange("p g t r -> p (g t) r"), in0=dis_x[:].rearrange("p g (t r) -> p (g t) r", r=4),
-                    in1=pick[:].unsqueeze(1).to_broadcast([P, 16, 4]), op=ALU.mult)
-                nc.vector.tensor_reduce(out=dis_j[:].rearrange("p g t -> p (g t)"), in_=dis_p[:].rearrange("p g t r -> p (g t) r"), axis=mybir.AxisListType.X, op=ALU.add)
-                transpose_w(0)
-                transpose_w(1)
-            if r == 2:
-                e_w("s", 0)
-                e_w("v", 1)
-                quantize("w", E4M3, "w", 1, src=w_grp[:])
-                dy_pass(1, 0)
-            if r > 1:
-                dy_pass(1, r - 1)
-            q_adj(0, r)
-            mask(r)
-        for r in range(2, RG):
-            adj_tile(1, r)
+            load_z2(r)
+            load_g(r)
+            load_adj(0, r)
+        load_w()
+        for r in range(2):
             load_adj(1, r)
+
+        for r in range(RG):
+            md(r)
+            int_adj("s", 0, r)
+            if r > 0:
+                q_adj(0, r - 1)
+                dy_pass(0, r - 1)
+            if r == 2:
+                dis_j_pick()
+            dz2(r)
+            q_dz2(r)
+        q_adj(0, 3)
+        transpose_w(0)
+        transpose_w(1)
+        e_w("s", 0)
+        e_w("s", 1)
+        dy_pass(0, 3)
+        int_adj("v", 1, 0)
+        for r in range(2, RG):
+            load_adj(1, r)
+        for r in range(RG):
+            load_adj(2, r)
         for g in range(RG):
             load_h(g)
 
-        int_adj("v", 2, 0)
-        q_dz2(3)
-        q_adj(1, 3)
-        dy_pass(0, 3)
-        dy_pass(1, 3)
-        for t in range(4):
-            e1("s", 0, t)
-        q_adj(2, 0)
-        int_adj("v", 2, 1)
-        transpose_dz1(0, 0)
-        transpose_dz1(0, 1)
-        e2("s", 0, 0)
-        e2("s", 0, 1)
-        int_dz1("v", 0)
-        q_adj(2, 1)
-        q_dz1t(0, 0)
-        q_dz1t(0, 1)
-        for t in range(4):
-            e1("s", 1, t)
-        q_dz1(0)
-        for t in range(2):
-            out0_pass(0, t)
-        int_adj("v", 2, 2)
-        dy_pass(2, 0)
-        dy_pass(2, 1)
-        e3("s", 0, 0)
-        e3("s", 0, 1)
-        for t in range(2, 4):
-            out0_pass(0, t)
-        transpose_dz1(1, 0)
-        transpose_dz1(1, 1)
-        e3("s", 0, 2)
-        e3("s", 0, 3)
-        e2("s", 1, 0)
-        e2("s", 1, 1)
-        int_dz1("v", 1)
-        q_adj(2, 2)
-        dy_pass(2, 2)
-        q_dz1t(1, 0)
-        q_dz1t(1, 1)
-        int_adj("s", 2, 3)
-        for t in range(2):
-            out0_pass(1, t)
-        q_dz1(1)
-        int_adj("v", 3, 0)
-        e3("s", 1, 0)
-        e3("s", 1, 1)
-        for t in range(2, 4):
-            out0_pass(1, t)
-        q_adj(2, 3)
-        dy_pass(2, 3)
-        e3("s", 1, 2)
-        e3("s", 1, 3)
-        int_adj("v", 3, 1)
-        q_adj(3, 0)
-        for t in range(4):
-            e1("s", 2, t)
-        int_h("v", 0)
-        q_adj(3, 1)
-        transpose_dz1(2, 0)
-        transpose_dz1(2, 1)
-        e2("s", 2, 0)
-        e2("s", 2, 1)
-        dy_pass(3, 0)
-        dy_pass(3, 1)
-        int_dz1("v", 2)
-        q_h(0)
-        int_adj("s", 3, 3)
-        q_dz1t(2, 0)
-        q_dz1t(2, 1)
-        int_adj("v", 3, 2)
-        q_dz1(2)
-        for t in range(2):
-            out0_pass(2, t)
-        int_h("v", 1)
-        q_adj(3, 2)
-        dy_pass(3, 2)
-        e3("s", 2, 0)
-        e3("s", 2, 1)
-        for t in range(2, 4):
-            out0_pass(2, t)
-        q_adj(3, 3)
-        dy_pass(3, 3)
-        q_h(1)
-        int_h("s", 3)
-        int_h("v", 2)
-        e3("s", 2, 2)
-        e3("s", 2, 3)
-        e1("s", 3, 0)
-        e1("v", 3, 1)
-        e1("s", 3, 2)
-        e1("v", 3, 3)
-        q_h(2)
-        transpose_dz1(3, 0)
-        transpose_dz1(3, 1)
-        for g in range(2):
-            for e in range(4):
-                out1_pass(e, g)
-        for e in range(4):
-            out1_pass(e, 2)
-        e2("s", 3, 0)
-        e2("s", 3, 1)
-        int_dz1("v", 3)
-        q_h(3)
-        q_dz1t(3, 0)
-        q_dz1t(3, 1)
-        q_dz1(3)
-        for t in range(2):
-            out0_pass(3, t)
+        fill_int = [lambda e, r: int_adj(e, 1, r), lambda e, r: int_adj(e, 2, r), lambda e, r: int_adj(e, 3, r), int_h]
+        fill_q = [lambda r: q_adj(1, r), lambda r: q_adj(2, r), lambda r: q_adj(3, r), q_h]
+
+        for k in range(4):
+            for t in range(4):
+                e1("s", k, t)
+            if k > 0:
+                fill_int[k]("v", 0)
+            fill_int[k]("v", 1)
+            fill_q[k](0)
+            transpose_dz1(k, 0)
+            transpose_dz1(k, 1)
+            if k == 0:
+                q_w()
+            if k < 3:
+                dy_pass(k + 1, 0)
+            e2("s", k, 0)
+            e2("s", k, 1)
+            fill_int[k]("v", 2)
+            q_dz1t(k, 0)
+            q_dz1t(k, 1)
+            for t in range(4):
+                out0_pass(k, t)
+            fill_int[k]("s", 3)
+            fill_q[k](1)
+            if k < 3:
+                dy_pass(k + 1, 1)
+            if k == 3:
+                for g in range(2):
+                    for e in range(4):
+                        out1_pass(e, g)
+                int_dz1("v", k)
+            fill_q[k](2)
+            if k == 3:
+                for e in range(4):
+                    out1_pass(e, 2)
+                q_dz1(3)
+            else:
+                dy_pass(k + 1, 2)
+            fill_q[k](3)
+            if k < 3:
+                dy_pass(k + 1, 3)
+                int_dz1("v", k)
+                q_dz1(k)
+            for t in range(4):
+                e3("s" if k < 3 else "svsv"[t], k, t)
         for e in range(4):
             out1_pass(e, 3)
-        e3("s", 3, 0)
-        e3("v", 3, 1)
-        for t in range(2, 4):
-            out0_pass(3, t)
-        e4("s", 0)
-        e4("v", 1)
-        e4("s", 2)
-        e4("v", 3)
-        e3("s", 3, 2)
-        e3("v", 3, 3)
+        for e in range(4):
+            e4("sv"[e % 2], e)

@@ -36,15 +36,16 @@ def tile_gcnclassifer_pa_v_kernel(tc, h_enc, adj, gcn1_w, gcn1_b, dis, z2, grad_
         make_identity(nc, ident[:])
         dummy = const.tile([P, 8], F32, name="dummy")
         nc.vector.memset(dummy[:], 0.0)
+        dis_i = const.tile([P, RG, K4], F32, name="dis_i")
+        nc.scalar.dma_start(out=dis_i[:], in_=dis.rearrange("(g p i) -> p g i", g=RG, i=K4))
         nc.scalar.activation(out=dummy[:, 0:1], in_=dummy[:, 1:2], func=COPY)
 
         def bank(b, name):
             return psum.tile([P, G], F32, name=name, tag="b%d" % b)
 
-        dis_i = const.tile([P, RG, K4], F32, name="dis_i")
         dis_j = const.tile([P, RG, 4], F32, name="dis_j")
         dis_x = const.tile([P, RG, 16], F32, name="dis_x")
-        dis_p = const.tile([P, RG, 4, 4], F32, name="dis_p")
+        dis_q = const.tile([P, RG, 4, 4], F32, name="dis_q")
         pick = const.tile([P, 4], F32, name="pick")
         z2_raw, g_raw, adj_raw, h_raw = {}, {}, {}, {}
 
@@ -55,7 +56,12 @@ def tile_gcnclassifer_pa_v_kernel(tc, h_enc, adj, gcn1_w, gcn1_b, dis, z2, grad_
 
         def load_z2(r):
             t = rawp.tile([P, K4, G], F32, name="z2_raw", tag="z2", bufs=4)
-            nc.sync.dma_start(out=t[:], in_=z2[r * G : (r + 1) * G, :].rearrange("(p i) c -> p i c", i=K4))
+            src = z2[r * G : (r + 1) * G, :].rearrange("(p i) c -> p i c", i=K4)
+            if r == 0:
+                nc.sync.dma_start(out=t[:, 0:2, :], in_=src[:, 0:2, :])
+                nc.sync.dma_start(out=t[:, 2:4, :], in_=src[:, 2:4, :])
+            else:
+                nc.sync.dma_start(out=t[:], in_=src)
             z2_raw[r] = t
 
         def load_adj(q, r):
@@ -103,7 +109,7 @@ def tile_gcnclassifer_pa_v_kernel(tc, h_enc, adj, gcn1_w, gcn1_b, dis, z2, grad_
         def int_adj(eng, q, r):
             raw = adj_raw[q, r]
             dst = stage_tile(("adj", q, r))
-            copy(eng, dst[:].rearrange("p (t a r i) -> p t a i r", t=4, r=4, i=K4), raw.rearrange("p i (a t r) -> p t a i r", t=4, r=4))
+            copy(eng, dst[:].rearrange("p (t a r i) -> p a t i r", t=4, r=4, i=K4), raw.rearrange("p i (a t r) -> p a t i r", t=4, r=4))
 
         def q_adj(q, r):
             quantize(("adj", q, r), E4M3, "adj", 8)
@@ -216,12 +222,6 @@ def tile_gcnclassifer_pa_v_kernel(tc, h_enc, adj, gcn1_w, gcn1_b, dis, z2, grad_
             copy(eng, o[:], o1[e][:])
             nc.sync.dma_start(out=out_1[e * P : (e + 1) * P, :], in_=o[:])
 
-        def dis_j_pick():
-            nc.vector.tensor_tensor(
-                out=dis_p[:].rearrange("p g t r -> p (g t) r"), in0=dis_x[:].rearrange("p g (t r) -> p (g t) r", r=4),
-                in1=pick[:].unsqueeze(1).to_broadcast([P, 16, 4]), op=ALU.mult)
-            nc.vector.tensor_reduce(out=dis_j[:].rearrange("p g t -> p (g t)"), in_=dis_p[:].rearrange("p g t r -> p (g t) r"), axis=mybir.AxisListType.X, op=ALU.add)
-
         def transpose_w(pair):
             x = bank(6 + pair, "xw")
             xt["w", pair] = x
@@ -238,12 +238,19 @@ def tile_gcnclassifer_pa_v_kernel(tc, h_enc, adj, gcn1_w, gcn1_b, dis, z2, grad_
         def q_w():
             quantize("w", E4M3, "w", 1, src=w_grp[:])
 
+        def load_dis_x():
+            for g in range(RG):
+                src = dis[g * G : (g + 1) * G].rearrange("(a x) -> a x", x=16)
+                nc.scalar.dma_start(out=dis_x[:, g, :], in_=src.unsqueeze(1).to_broadcast([32, 4, 16]))
+
+        def dis_j_pick():
+            nc.vector.tensor_reduce(out=pick[:], in_=ident[:].rearrange("p (a r) -> p r a", r=4), axis=mybir.AxisListType.X, op=ALU.add)
+            nc.vector.tensor_tensor(
+                out=dis_q[:].rearrange("p g t r -> p (g t) r"), in0=dis_x[:].rearrange("p g (t r) -> p (g t) r", r=4),
+                in1=pick[:].unsqueeze(1).to_broadcast([P, 16, 4]), op=ALU.mult)
+            nc.vector.tensor_reduce(out=dis_j[:].rearrange("p g t -> p (g t)"), in_=dis_q[:].rearrange("p g t r -> p (g t) r"), axis=mybir.AxisListType.X, op=ALU.add)
+
         ctx.enter_context(tc.manual_schedule())
-        nc.scalar.dma_start(out=dis_i[:], in_=dis.rearrange("(g p i) -> p g i", g=RG, i=K4))
-        for g in range(RG):
-            src = dis[g * G : (g + 1) * G].rearrange("(a x) -> a x", x=16)
-            nc.scalar.dma_start(out=dis_x[:, g, :], in_=src.unsqueeze(1).to_broadcast([32, 4, 16]))
-        nc.vector.tensor_reduce(out=pick[:], in_=ident[:].rearrange("p (a r) -> p r a", r=4), axis=mybir.AxisListType.X, op=ALU.add)
         for r in range(RG):
             load_z2(r)
             load_g(r)
@@ -255,6 +262,8 @@ def tile_gcnclassifer_pa_v_kernel(tc, h_enc, adj, gcn1_w, gcn1_b, dis, z2, grad_
         for r in range(RG):
             md(r)
             int_adj("s", 0, r)
+            if r == 0:
+                load_dis_x()
             if r > 0:
                 q_adj(0, r - 1)
                 dy_pass(0, r - 1)
@@ -276,53 +285,72 @@ def tile_gcnclassifer_pa_v_kernel(tc, h_enc, adj, gcn1_w, gcn1_b, dis, z2, grad_
         for g in range(RG):
             load_h(g)
 
-        fill_int = [lambda e, r: int_adj(e, 1, r), lambda e, r: int_adj(e, 2, r), lambda e, r: int_adj(e, 3, r), int_h]
-        fill_q = [lambda r: q_adj(1, r), lambda r: q_adj(2, r), lambda r: q_adj(3, r), q_h]
 
-        for k in range(4):
-            for t in range(4):
-                e1("s", k, t)
+        for k in range(3):
             if k > 0:
-                fill_int[k]("v", 0)
-            fill_int[k]("v", 1)
-            fill_q[k](0)
-            transpose_dz1(k, 0)
-            transpose_dz1(k, 1)
-            if k == 0:
+                int_adj("v", k + 1, 0)
+            for pair in range(2):
+                e1("s", k, 2 * pair)
+                e1("s", k, 2 * pair + 1)
+                transpose_dz1(k, pair)
+            if k > 0:
+                q_dz1(k - 1)
+            else:
                 q_w()
-            if k < 3:
-                dy_pass(k + 1, 0)
+            int_adj("v", k + 1, 1)
+            q_adj(k + 1, 0)
+            int_adj("v", k + 1, 2)
+            q_adj(k + 1, 1)
             e2("s", k, 0)
+            dy_pass(k + 1, 0)
             e2("s", k, 1)
-            fill_int[k]("v", 2)
+            int_adj("s", k + 1, 3)
             q_dz1t(k, 0)
             q_dz1t(k, 1)
+            q_adj(k + 1, 2)
+            dy_pass(k + 1, 1)
             for t in range(4):
                 out0_pass(k, t)
-            fill_int[k]("s", 3)
-            fill_q[k](1)
-            if k < 3:
-                dy_pass(k + 1, 1)
-            if k == 3:
-                for g in range(2):
-                    for e in range(4):
-                        out1_pass(e, g)
-                int_dz1("v", k)
-            fill_q[k](2)
-            if k == 3:
-                for e in range(4):
-                    out1_pass(e, 2)
-                q_dz1(3)
-            else:
-                dy_pass(k + 1, 2)
-            fill_q[k](3)
-            if k < 3:
-                dy_pass(k + 1, 3)
-                int_dz1("v", k)
-                q_dz1(k)
+            dy_pass(k + 1, 2)
+            int_dz1("v", k)
+            q_adj(k + 1, 3)
+            dy_pass(k + 1, 3)
             for t in range(4):
-                e3("s" if k < 3 else "svsv"[t], k, t)
+                e3("s", k, t)
+
+
+        int_h("v", 0)
+        for t in range(3):
+            e1("s", 3, t)
+        int_h("v", 1)
+        e1("v", 3, 3)
+        int_dz1("s", 3)
+        transpose_dz1(3, 0)
+        q_h(0)
+        q_h(1)
+        for g in range(2):
+            for e in range(4):
+                out1_pass(e, g)
+            if g == 0:
+                transpose_dz1(3, 1)
+        e2("v", 3, 0)
+        int_h("v", 2)
+        q_dz1t(3, 0)
+        e2("s", 3, 1)
+        q_h(2)
+        q_dz1t(3, 1)
+        for t in range(4):
+            out0_pass(3, t)
+        q_dz1(2)
+        e3("v", 3, 1)
+        int_h("s", 3)
+        q_dz1(3)
+        e3("s", 3, 0)
+        e3("s", 3, 2)
+        for e in range(4):
+            out1_pass(e, 2)
+        q_h(3)
+        e3("s", 3, 3)
         for e in range(4):
             out1_pass(e, 3)
-        for e in range(4):
-            e4("sv"[e % 2], e)
+            e4("vvsv"[e], e)

@@ -157,10 +157,12 @@ def tile_gcnclassifer_pa_v_kernel(tc, h_enc, adj, gcn1_w, gcn1_b, dis, z2, grad_
             if t == 0:
                 dz1[q] = work.tile([P, 4, G], BF16, name="dz1", tag="dz1", bufs=2, align_bytes=64)
             s = dis_j[:, q, t : t + 1]
+            dst = dz1[q][:, t, :].rearrange("p (u w e) -> p u w e", u=2, e=2)
+            src = dy[q, t][:].rearrange("p (w u e) -> p u w e", u=2, e=2)
             if eng == "v":
-                nc.vector.tensor_scalar(out=dz1[q][:, t, :], in0=dy[q, t][:], scalar1=s, scalar2=None, op0=ALU.mult)
+                nc.vector.tensor_scalar(out=dst, in0=src, scalar1=s, scalar2=None, op0=ALU.mult)
             else:
-                nc.scalar.activation(out=dz1[q][:, t, :], in_=dy[q, t][:], func=COPY, scale=s)
+                nc.scalar.activation(out=dst, in_=src, func=COPY, scale=s)
 
         def int_dz1(eng, q):
             dst = stage_tile(("dz1", q))
@@ -178,7 +180,7 @@ def tile_gcnclassifer_pa_v_kernel(tc, h_enc, adj, gcn1_w, gcn1_b, dis, z2, grad_
             for s in range(2):
                 words = dz1[q][:, 2 * pair + s, :].bitcast(F32)
                 for u in range(2):
-                    nc.tensor.transpose(xv[:, s, u, :], words[:, u::2], ident[:])
+                    nc.tensor.transpose(xv[:, s, u, :], words[:, u * P : (u + 1) * P], ident[:])
 
         def e2(eng, q, pair):
             t = work.tile([P, 8 * P], BF16, name="dz1t", tag="dz1t", bufs=4, align_bytes=64)
@@ -219,7 +221,7 @@ def tile_gcnclassifer_pa_v_kernel(tc, h_enc, adj, gcn1_w, gcn1_b, dis, z2, grad_
 
         def e4(eng, e):
             o = work.tile([P, G], F32, name="o_sb", tag="o_sb", bufs=8)
-            copy(eng, o[:], o1[e][:])
+            copy(eng, o[:].rearrange("p (w u e) -> p w u e", u=2, e=2), o1[e][:].rearrange("p (u w e) -> p w u e", u=2, e=2))
             nc.sync.dma_start(out=out_1[e * P : (e + 1) * P, :], in_=o[:])
 
         def transpose_w(pair):
@@ -288,69 +290,72 @@ def tile_gcnclassifer_pa_v_kernel(tc, h_enc, adj, gcn1_w, gcn1_b, dis, z2, grad_
 
         for k in range(3):
             if k > 0:
-                int_adj("v", k + 1, 0)
-            for pair in range(2):
-                e1("s", k, 2 * pair)
-                e1("s", k, 2 * pair + 1)
-                transpose_dz1(k, pair)
-            if k > 0:
                 q_dz1(k - 1)
-            else:
-                q_w()
+                int_adj("v", k + 1, 0)
+            e1("s", k, 0)
+            e1("s", k, 1)
+            transpose_dz1(k, 0)
             int_adj("v", k + 1, 1)
             q_adj(k + 1, 0)
+            e1("s", k, 2)
+            e1("s", k, 3)
+            transpose_dz1(k, 1)
             int_adj("v", k + 1, 2)
-            q_adj(k + 1, 1)
             e2("s", k, 0)
-            dy_pass(k + 1, 0)
             e2("s", k, 1)
-            int_adj("s", k + 1, 3)
             q_dz1t(k, 0)
+            if k == 0:
+                q_w()
+            q_adj(k + 1, 1)
             q_dz1t(k, 1)
-            q_adj(k + 1, 2)
-            dy_pass(k + 1, 1)
+            int_adj("s", k + 1, 3)
+            dy_pass(k + 1, 0)
             for t in range(4):
                 out0_pass(k, t)
-            dy_pass(k + 1, 2)
+            q_adj(k + 1, 2)
             int_dz1("v", k)
             q_adj(k + 1, 3)
-            dy_pass(k + 1, 3)
+            for r in range(1, RG):
+                dy_pass(k + 1, r)
             for t in range(4):
                 e3("s", k, t)
 
 
         int_h("v", 0)
-        for t in range(3):
-            e1("s", 3, t)
+        e1("s", 3, 0)
+        e1("s", 3, 1)
         int_h("v", 1)
-        e1("v", 3, 3)
-        int_dz1("s", 3)
         transpose_dz1(3, 0)
         q_h(0)
+        e1("s", 3, 2)
+        e1("s", 3, 3)
         q_h(1)
-        for g in range(2):
-            for e in range(4):
-                out1_pass(e, g)
-            if g == 0:
-                transpose_dz1(3, 1)
+        transpose_dz1(3, 1)
         e2("v", 3, 0)
         int_h("v", 2)
+        for e in range(4):
+            out1_pass(e, 0)
+        e2("v", 3, 1)
         q_dz1t(3, 0)
-        e2("s", 3, 1)
-        q_h(2)
+        out0_pass(3, 0)
+        out0_pass(3, 1)
         q_dz1t(3, 1)
-        for t in range(4):
-            out0_pass(3, t)
         q_dz1(2)
-        e3("v", 3, 1)
         int_h("s", 3)
+        q_h(2)
+        out0_pass(3, 2)
+        out0_pass(3, 3)
+        e3("v", 3, 0)
+        int_dz1("s", 3)
+        q_h(3)
+        for e in range(4):
+            out1_pass(e, 1)
         q_dz1(3)
-        e3("s", 3, 0)
-        e3("s", 3, 2)
         for e in range(4):
             out1_pass(e, 2)
-        q_h(3)
+        e3("s", 3, 2)
         e3("s", 3, 3)
+        e3("v", 3, 1)
         for e in range(4):
             out1_pass(e, 3)
-            e4("vvsv"[e], e)
+            e4("svsv"[e], e)

from contextlib import ExitStack

import concourse.mybir as mybir
from concourse.masks import make_identity

N, E, H = 2048, 512, 512

FLOPS = 2 * N * N * H + 2 * N * H * E + 2 * N * E * H
BYTES = 2 * (N * E + N * N + E * H + N * H) + 4 * (N + N * H) + 4 * (N * E + E * H)

F32 = mybir.dt.float32
BF16 = mybir.dt.bfloat16
U32 = mybir.dt.uint32
U8 = mybir.dt.uint8
E4M3 = mybir.dt.float8_e4m3fn_x4
E5M2 = mybir.dt.float8_e5m2_x4
ALU = mybir.AluOpType
COPY = mybir.ActivationFunctionType.Copy

P = 128
K4 = 4
G = 512
RG = N // G


def tile_gcnclassifer_pa_v_kernel(tc, h_enc, adj, gcn1_w, gcn1_b, dis, z2, grad_out, out_0, out_1):
    nc = tc.nc
    with ExitStack() as ctx:
        const = ctx.enter_context(tc.tile_pool(name="const", bufs=1))
        rawp = ctx.enter_context(tc.tile_pool(name="rawp", bufs=4))
        work = ctx.enter_context(tc.tile_pool(name="work", bufs=2))
        code = ctx.enter_context(tc.tile_pool(name="code", bufs=4))
        psum = ctx.enter_context(tc.psum_pool(name="psum", bufs=1))

        ident = const.tile([P, P], F32, name="ident")
        make_identity(nc, ident[:])
        dummy = const.tile([P, 8], F32, name="dummy")
        nc.vector.memset(dummy[:], 0.0)
        dis_i = const.tile([P, RG, K4], F32, name="dis_i")
        nc.scalar.dma_start(out=dis_i[:], in_=dis.rearrange("(g p i) -> p g i", g=RG, i=K4))
        nc.scalar.activation(out=dummy[:, 0:1], in_=dummy[:, 1:2], func=COPY)

        def bank(b, name):
            return psum.tile([P, G], F32, name=name, tag="b%d" % b)

        dis_j = const.tile([P, RG, 4], F32, name="dis_j")
        dis_x = const.tile([P, RG, 16], F32, name="dis_x")
        dis_q = const.tile([P, RG, 4, 4], F32, name="dis_q")
        pick = const.tile([P, 4], F32, name="pick")
        z2_raw, g_raw, adj_raw, h_raw = {}, {}, {}, {}

        def load_g(r):
            t = rawp.tile([P, K4, G], BF16, name="g_raw", tag="gh", bufs=4)
            nc.sync.dma_start(out=t[:], in_=grad_out[r * G : (r + 1) * G, :].rearrange("(p i) c -> p i c", i=K4))
            g_raw[r] = t

        def load_z2(r):
            t = rawp.tile([P, K4, G], F32, name="z2_raw", tag="z2", bufs=4)
            src = z2[r * G : (r + 1) * G, :].rearrange("(p i) c -> p i c", i=K4)
            if r == 0:
                nc.sync.dma_start(out=t[:, 0:2, :], in_=src[:, 0:2, :])
                nc.sync.dma_start(out=t[:, 2:4, :], in_=src[:, 2:4, :])
            else:
                nc.sync.dma_start(out=t[:], in_=src)
            z2_raw[r] = t

        def load_adj(q, r):
            n = 1 if q < 2 else 2
            t = rawp.tile([P, K4, n * G], BF16, name="adj_raw", tag="adj%d" % n, bufs=(6 if n == 1 else 4))
            rows = adj[r * G : (r + 1) * G, q * G : (q + n) * G]
            nc.sync.dma_start(out=t[:], in_=rows.rearrange("(p i) c -> p i c", i=K4))
            for s in range(n):
                adj_raw[q + s, r] = t[:, :, s * G : (s + 1) * G]

        w_raw = const.tile([P, 4, H], BF16, name="w_raw", align_bytes=64)
        w_grp = const.tile([P, 4 * E], BF16, name="w_grp", align_bytes=64)

        def load_w():
            nc.sync.dma_start(out=w_raw[:], in_=gcn1_w.rearrange("(e p) c -> p e c", p=P))

        def load_h(g):
            t = rawp.tile([P, K4, G], BF16, name="h_raw", tag="gh", bufs=4)
            rows = h_enc[g * G : (g + 1) * G, :].rearrange("(a t r) c -> t a r c", t=4, r=4)
            for s in range(4):
                nc.sync.dma_start(out=t[:, s, :], in_=rows[s])
            h_raw[g] = t

        stage = {}

        def stage_tile(key):
            t = work.tile([P, 4 * G], BF16, name="stage", tag="stage", bufs=7, align_bytes=64)
            stage[key] = t
            return t

        codes = {}

        def quantize(key, fmt, tag, bufs, width=G, src=None):
            cw = code.tile([P, width], U32, name="cw_" + tag, tag="c_" + tag, bufs=bufs, align_bytes=64)
            sc = code.tile([P, width], U8, name="sc_" + tag, tag="s_" + tag, bufs=bufs, align_bytes=64)
            nc.vector.quantize_mx(out=cw[:].bitcast(fmt), scales=sc[:], in_=(stage[key][:] if src is None else src))
            codes[key] = (cw, sc)

        def copy(eng, out, in_):
            if eng == "v":
                nc.vector.tensor_copy(out=out, in_=in_)
            else:
                nc.scalar.copy(out=out, in_=in_)

        def int_adj(eng, q, r):
            raw = adj_raw[q, r]
            dst = stage_tile(("adj", q, r))
            copy(eng, dst[:].rearrange("p (t a r i) -> p a t i r", t=4, r=4, i=K4), raw.rearrange("p i (a t r) -> p a t i r", t=4, r=4))

        def q_adj(q, r):
            quantize(("adj", q, r), E4M3, "adj", 8)

        def int_h(eng, g):
            dst = stage_tile(("h", g))
            copy(eng, dst[:].rearrange("p (c i t) -> p c t i", i=4, t=K4), h_raw[g][:].rearrange("p t (c i) -> p c t i", i=4))

        def q_h(g):
            quantize(("h", g), E4M3, "h", 4)

        def md(r):
            for i in range(K4):
                nc.vector.tensor_scalar(
                    out=z2_raw[r][:, i, :], in0=z2_raw[r][:, i, :], scalar1=0.0, scalar2=dis_i[:, r, i : i + 1], op0=ALU.is_gt, op1=ALU.mult)

        def dz2(r):
            dst = stage_tile(("dz2", r))
            nc.vector.tensor_tensor(
                out=dst[:].rearrange("p (c i t) -> p c t i", i=4, t=K4),
                in0=z2_raw[r][:].rearrange("p t (c i) -> p c t i", i=4),
                in1=g_raw[r][:].rearrange("p t (c i) -> p c t i", i=4),
                op=ALU.mult)

        def q_dz2(r):
            quantize(("dz2", r), E5M2, "dz2", 4)

        dy = {}
        dy_bank = [0, 4, 0, 4]

        def dy_pass(q, r):
            for t in range(4):
                if r == 0:
                    dy[q, t] = bank(dy_bank[q] + t, "dy")
                a, asc = codes["adj", q, r]
                b, bsc = codes["dz2", r]
                m = slice(t * P, (t + 1) * P)
                nc.tensor.matmul_mx(
                    out=dy[q, t][:], lhsT=a[:, m].bitcast(E4M3), lhsT_scale=asc[:, m],
                    rhs=b[:].bitcast(E5M2), rhs_scale=bsc[:], start=(r == 0), stop=(r == RG - 1))

        dz1 = {}

        def e1(eng, q, t):
            if t == 0:
                dz1[q] = work.tile([P, 4, G], BF16, name="dz1", tag="dz1", bufs=2, align_bytes=64)
            s = dis_j[:, q, t : t + 1]
            dst = dz1[q][:, t, :].rearrange("p (u w e) -> p u w e", u=2, e=2)
            src = dy[q, t][:].rearrange("p (w u e) -> p u w e", u=2, e=2)
            if eng == "v":
                nc.vector.tensor_scalar(out=dst, in0=src, scalar1=s, scalar2=None, op0=ALU.mult)
            else:
                nc.scalar.activation(out=dst, in_=src, func=COPY, scale=s)

        def int_dz1(eng, q):
            dst = stage_tile(("dz1", q))
            copy(eng, dst[:].rearrange("p (c i t) -> p c t i", i=4, t=4), dz1[q][:].rearrange("p t (c i) -> p c t i", i=4))

        def q_dz1(q):
            quantize(("dz1", q), E5M2, "dz1", 4)

        xt = {}

        def transpose_dz1(q, pair):
            x = bank(dy_bank[q] + pair, "xt")
            xt[q, pair] = x
            xv = x[:].rearrange("p (s u m) -> p s u m", s=2, u=2)
            for s in range(2):
                words = dz1[q][:, 2 * pair + s, :].bitcast(F32)
                for u in range(2):
                    nc.tensor.transpose(xv[:, s, u, :], words[:, u * P : (u + 1) * P], ident[:])

        def e2(eng, q, pair):
            t = work.tile([P, 8 * P], BF16, name="dz1t", tag="dz1t", bufs=4, align_bytes=64)
            copy(eng, t[:].bitcast(F32).rearrange("p (s m u) -> p s m u", s=2, u=2), xt[q, pair][:].rearrange("p (s u m) -> p s m u", s=2, u=2))
            stage["dz1t", q, pair] = t

        def q_dz1t(q, pair):
            quantize(("dz1t", q, pair), E5M2, "dz1t", 4, width=2 * P)

        o0 = {}

        def out0_pass(q, t):
            o0[q, t] = bank(dy_bank[q] + (t + 2) % 4, "o0")
            a, asc = codes["dz1t", q, t // 2]
            b, bsc = codes["w"]
            m = slice((t % 2) * P, (t % 2 + 1) * P)
            nc.tensor.matmul_mx(
                out=o0[q, t][:], lhsT=a[:, m].bitcast(E5M2), lhsT_scale=asc[:, m],
                rhs=b[:].bitcast(E4M3), rhs_scale=bsc[:], start=True, stop=True)

        def e3(eng, q, t):
            o = work.tile([P, G], F32, name="o_sb", tag="o_sb", bufs=8)
            copy(eng, o[:], o0[q, t][:])
            rows = out_0[q * G : (q + 1) * G, :].rearrange("(a t r) c -> t a r c", t=4, r=4)
            nc.sync.dma_start(out=rows[t], in_=o[:])

        o1 = {}

        def out1_pass(e, g):
            if g == 0:
                o1[e] = bank(e, "o1")
            a, asc = codes["h", g]
            b, bsc = codes["dz1", g]
            m = slice(e * P, (e + 1) * P)
            nc.tensor.matmul_mx(
                out=o1[e][:], lhsT=a[:, m].bitcast(E4M3), lhsT_scale=asc[:, m],
                rhs=b[:].bitcast(E5M2), rhs_scale=bsc[:], start=(g == 0), stop=(g == RG - 1))

        def e4(eng, e):
            o = work.tile([P, G], F32, name="o_sb", tag="o_sb", bufs=8)
            copy(eng, o[:].rearrange("p (w u e) -> p w u e", u=2, e=2), o1[e][:].rearrange("p (u w e) -> p w u e", u=2, e=2))
            nc.sync.dma_start(out=out_1[e * P : (e + 1) * P, :], in_=o[:])

        def transpose_w(pair):
            x = bank(6 + pair, "xw")
            xt["w", pair] = x
            xv = x[:].rearrange("p (s u m) -> p s u m", s=2, u=2)
            for s in range(2):
                words = w_raw[:, 2 * pair + s, :].bitcast(F32)
                for u in range(2):
                    nc.tensor.transpose(xv[:, s, u, :], words[:, u::2], ident[:])

        def e_w(eng, pair):
            dst = w_grp[:].bitcast(F32)[:, pair * 512 : (pair + 1) * 512]
            copy(eng, dst.rearrange("p (s m u) -> p s m u", s=2, u=2), xt["w", pair][:].rearrange("p (s u m) -> p s m u", s=2, u=2))

        def q_w():
            quantize("w", E4M3, "w", 1, src=w_grp[:])

        def load_dis_x():
            for g in range(RG):
                src = dis[g * G : (g + 1) * G].rearrange("(a x) -> a x", x=16)
                nc.scalar.dma_start(out=dis_x[:, g, :], in_=src.unsqueeze(1).to_broadcast([32, 4, 16]))

        def dis_j_pick():
            nc.vector.tensor_reduce(out=pick[:], in_=ident[:].rearrange("p (a r) -> p r a", r=4), axis=mybir.AxisListType.X, op=ALU.add)
            nc.vector.tensor_tensor(
                out=dis_q[:].rearrange("p g t r -> p (g t) r"), in0=dis_x[:].rearrange("p g (t r) -> p (g t) r", r=4),
                in1=pick[:].unsqueeze(1).to_broadcast([P, 16, 4]), op=ALU.mult)
            nc.vector.tensor_reduce(out=dis_j[:].rearrange("p g t -> p (g t)"), in_=dis_q[:].rearrange("p g t r -> p (g t) r"), axis=mybir.AxisListType.X, op=ALU.add)

        ctx.enter_context(tc.manual_schedule())
        for r in range(RG):
            load_z2(r)
            load_g(r)
            load_adj(0, r)
        load_w()
        for r in range(2):
            load_adj(1, r)

        for r in range(RG):
            md(r)
            int_adj("s", 0, r)
            if r == 0:
                load_dis_x()
            if r > 0:
                q_adj(0, r - 1)
                dy_pass(0, r - 1)
            if r == 2:
                dis_j_pick()
            dz2(r)
            q_dz2(r)
        q_adj(0, 3)
        transpose_w(0)
        transpose_w(1)
        e_w("s", 0)
        e_w("s", 1)
        dy_pass(0, 3)
        int_adj("v", 1, 0)
        for r in range(2, RG):
            load_adj(1, r)
        for r in range(RG):
            load_adj(2, r)
        for g in range(RG):
            load_h(g)


        for k in range(3):
            if k > 0:
                q_dz1(k - 1)
                int_adj("v", k + 1, 0)
            e1("s", k, 0)
            e1("s", k, 1)
            transpose_dz1(k, 0)
            int_adj("v", k + 1, 1)
            q_adj(k + 1, 0)
            e1("s", k, 2)
            e1("s", k, 3)
            transpose_dz1(k, 1)
            int_adj("v", k + 1, 2)
            e2("s", k, 0)
            e2("s", k, 1)
            q_dz1t(k, 0)
            if k == 0:
                q_w()
            q_adj(k + 1, 1)
            q_dz1t(k, 1)
            int_adj("s", k + 1, 3)
            dy_pass(k + 1, 0)
            for t in range(4):
                out0_pass(k, t)
            q_adj(k + 1, 2)
            int_dz1("v", k)
            q_adj(k + 1, 3)
            for r in range(1, RG):
                dy_pass(k + 1, r)
            for t in range(4):
                e3("s", k, t)


        int_h("v", 0)
        e1("s", 3, 0)
        e1("s", 3, 1)
        int_h("v", 1)
        transpose_dz1(3, 0)
        q_h(0)
        e1("s", 3, 2)
        e1("s", 3, 3)
        q_h(1)
        transpose_dz1(3, 1)
        e2("v", 3, 0)
        int_h("v", 2)
        for e in range(4):
            out1_pass(e, 0)
        e2("v", 3, 1)
        q_dz1t(3, 0)
        out0_pass(3, 0)
        out0_pass(3, 1)
        q_dz1t(3, 1)
        q_dz1(2)
        int_h("s", 3)
        q_h(2)
        out0_pass(3, 2)
        out0_pass(3, 3)
        e3("v", 3, 0)
        int_dz1("s", 3)
        q_h(3)
        for e in range(4):
            out1_pass(e, 1)
        q_dz1(3)
        for e in range(4):
            out1_pass(e, 2)
        e3("s", 3, 2)
        e3("s", 3, 3)
        e3("v", 3, 1)
        for e in range(4):
            out1_pass(e, 3)
            e4("svsv"[e], e)
